import numpy as np
import ml_dtypes

BF16 = ml_dtypes.bfloat16


def bf(x):
    return np.asarray(x, np.float32).astype(BF16)


def f32(x):
    return np.asarray(x, np.float32)


def f64(x):
    return np.asarray(x).astype(np.float64)


def striped(idx):
    return np.tile(idx.reshape(-1, 16).T, (8, 1))


D, S, M, N = 128, 1024, 128, 256
SCALE = 0.125


def setup_inputs():
    return {"table": bf(np.random.standard_normal((D, S))), "w": bf(np.random.standard_normal((D, M))), "v": bf(np.random.standard_normal((D, N))), "offs": striped(np.random.permutation(S)[:N])}


def reference(table, w, v, offs):
    idx = offs[:16].T.reshape(-1)
    a = SCALE * (f64(w).T @ f64(table)[:, idx])
    e = np.exp(a - a.max(axis=1, keepdims=True))
    p = e / e.sum(axis=1, keepdims=True)
    return p @ f64(v).T

@@ -1,0 +1,69 @@
+import concourse.mybir as mybir
+from concourse.masks import make_identity
+
+P = 128
+S = 1024
+M = 128
+N = 256
+D = 128
+HALVES = N // P
+SCALE = 0.125
+
+FLOPS = 2 * P * M * N + 2 * N * M * D
+
+BF16 = mybir.dt.bfloat16
+F32 = mybir.dt.float32
+U16 = mybir.dt.uint16
+
+
+def tile_nativesparseattentionlayer_kernel(tc, table, w, v, offs, out):
+    nc = tc.nc
+    with tc.tile_pool(name="held", bufs=1) as held, tc.psum_pool(name="psum", bufs=1) as psum:
+        offsets = held.tile([P, N // 16], U16, name="offsets")
+        nc.sync.dma_start(offsets[:], offs)
+        keys = held.tile([P, S], BF16, name="keys")
+        nc.sync.dma_start(keys[:], table)
+        queries = held.tile([P, M], BF16, name="queries")
+        nc.scalar.dma_start(queries[:], w)
+        values = held.tile([P, N], BF16, name="values")
+        nc.scalar.dma_start(values[:], v)
+
+        identity = held.tile([P, P], BF16, name="identity")
+        make_identity(nc, identity[:])
+
+        values_t = []
+        for h in range(HALVES):
+            flipped = psum.tile([P, D], BF16, name=f"values_t_psum{h}")
+            nc.tensor.transpose(flipped[:], values[:, h * P : (h + 1) * P], identity[:])
+            kept = held.tile([P, D], BF16, name=f"values_t{h}")
+            nc.vector.tensor_copy(kept[:], flipped[:])
+            values_t.append(kept)
+
+        scores = psum.tile([M, N], F32, name="scores")
+        nc.tensor.matmul(scores[:], queries[:], keys[:].indirect(offsets[:]), start=True, stop=True)
+
+        top = held.tile([M, 1], F32, name="top")
+        nc.vector.reduce_max(top[:], scores[:], axis=mybir.AxisListType.X)
+        shift = held.tile([M, 1], F32, name="shift")
+        nc.vector.tensor_scalar_mul(shift[:], top[:], -SCALE)
+        raised = held.tile([M, N], F32, name="raised")
+        total = held.tile([M, 1], F32, name="total")
+        nc.scalar.activation(
+            raised[:], scores[:], mybir.ActivationFunctionType.Exp, bias=shift[:], scale=SCALE, accum_out=total[:]
+        )
+        inverse = held.tile([M, 1], F32, name="inverse")
+        nc.vector.reciprocal(inverse[:], total[:])
+        probs = held.tile([M, N], BF16, name="probs")
+        nc.vector.tensor_scalar_mul(probs[:], raised[:], inverse[:])
+
+        result = psum.tile([M, D], F32, name="result")
+        for h in range(HALVES):
+            flipped = psum.tile([P, M], BF16, name=f"probs_t_psum{h}")
+            nc.tensor.transpose(flipped[:], probs[:, h * P : (h + 1) * P], identity[:])
+            probs_t = held.tile([P, M], BF16, name=f"probs_t{h}")
+            nc.vector.tensor_copy(probs_t[:], flipped[:])
+            nc.tensor.matmul(result[:], probs_t[:], values_t[h][:], start=(h == 0), stop=(h == HALVES - 1))
+
+        staged = held.tile([M, D], F32, name="staged")
+        nc.vector.tensor_copy(staged[:], result[:])
+        nc.sync.dma_start(out, staged[:])

@@ -19,25 +19,17 @@ U16 = mybir.dt.uint16
 def tile_nativesparseattentionlayer_kernel(tc, table, w, v, offs, out):
     nc = tc.nc
     with tc.tile_pool(name="held", bufs=1) as held, tc.psum_pool(name="psum", bufs=1) as psum:
+        keys = held.tile([P, S], BF16, name="keys")
+        nc.scalar.dma_start(keys[:], table)
         offsets = held.tile([P, N // 16], U16, name="offsets")
         nc.sync.dma_start(offsets[:], offs)
-        keys = held.tile([P, S], BF16, name="keys")
-        nc.sync.dma_start(keys[:], table)
         queries = held.tile([P, M], BF16, name="queries")
-        nc.scalar.dma_start(queries[:], w)
+        nc.sync.dma_start(queries[:], w)
         values = held.tile([P, N], BF16, name="values")
-        nc.scalar.dma_start(values[:], v)
+        nc.gpsimd.dma_start(values[:], v)
 
         identity = held.tile([P, P], BF16, name="identity")
         make_identity(nc, identity[:])
-
-        values_t = []
-        for h in range(HALVES):
-            flipped = psum.tile([P, D], BF16, name=f"values_t_psum{h}")
-            nc.tensor.transpose(flipped[:], values[:, h * P : (h + 1) * P], identity[:])
-            kept = held.tile([P, D], BF16, name=f"values_t{h}")
-            nc.vector.tensor_copy(kept[:], flipped[:])
-            values_t.append(kept)
 
         scores = psum.tile([M, N], F32, name="scores")
         nc.tensor.matmul(scores[:], queries[:], keys[:].indirect(offsets[:]), start=True, stop=True)
@@ -51,18 +43,34 @@ def tile_nativesparseattentionlayer_kernel(tc, table, w, v, offs, out):
         nc.scalar.activation(
             raised[:], scores[:], mybir.ActivationFunctionType.Exp, bias=shift[:], scale=SCALE, accum_out=total[:]
         )
+
+        values_t_psum = psum.tile([P, HALVES * D], BF16, name="values_t_psum")
+        for h in range(HALVES):
+            nc.tensor.transpose(values_t_psum[:, h * D : (h + 1) * D], values[:, h * P : (h + 1) * P], identity[:])
+        values_t = held.tile([P, HALVES * D], BF16, name="values_t")
+        nc.scalar.copy(values_t[:], values_t_psum[:])
+
         inverse = held.tile([M, 1], F32, name="inverse")
         nc.vector.reciprocal(inverse[:], total[:])
         probs = held.tile([M, N], BF16, name="probs")
         nc.vector.tensor_scalar_mul(probs[:], raised[:], inverse[:])
 
-        result = psum.tile([M, D], F32, name="result")
+        probs_t = []
         for h in range(HALVES):
             flipped = psum.tile([P, M], BF16, name=f"probs_t_psum{h}")
             nc.tensor.transpose(flipped[:], probs[:, h * P : (h + 1) * P], identity[:])
-            probs_t = held.tile([P, M], BF16, name=f"probs_t{h}")
-            nc.vector.tensor_copy(probs_t[:], flipped[:])
-            nc.tensor.matmul(result[:], probs_t[:], values_t[h][:], start=(h == 0), stop=(h == HALVES - 1))
+            kept = held.tile([P, M], BF16, name=f"probs_t{h}")
+            if h % 2 == 0:
+                nc.vector.tensor_copy(kept[:], flipped[:])
+            else:
+                nc.scalar.copy(kept[:], flipped[:])
+            probs_t.append(kept)
+
+        result = psum.tile([M, D], F32, name="result")
+        for h in range(HALVES):
+            nc.tensor.matmul(
+                result[:], probs_t[h][:], values_t[:, h * D : (h + 1) * D], start=(h == 0), stop=(h == HALVES - 1)
+            )
 
         staged = held.tile([M, D], F32, name="staged")
         nc.vector.tensor_copy(staged[:], result[:])

@@ -38,7 +38,7 @@ def tile_nativesparseattentionlayer_kernel(tc, table, w, v, offs, out):
         nc.vector.reduce_max(top[:], scores[:], axis=mybir.AxisListType.X)
         shift = held.tile([M, 1], F32, name="shift")
         nc.vector.tensor_scalar_mul(shift[:], top[:], -SCALE)
-        raised = held.tile([M, N], F32, name="raised")
+        raised = held.tile([M, N], BF16, name="raised")
         total = held.tile([M, 1], F32, name="total")
         nc.scalar.activation(
             raised[:], scores[:], mybir.ActivationFunctionType.Exp, bias=shift[:], scale=SCALE, accum_out=total[:]
@@ -52,26 +52,24 @@ def tile_nativesparseattentionlayer_kernel(tc, table, w, v, offs, out):
 
         inverse = held.tile([M, 1], F32, name="inverse")
         nc.vector.reciprocal(inverse[:], total[:])
-        probs = held.tile([M, N], BF16, name="probs")
-        nc.vector.tensor_scalar_mul(probs[:], raised[:], inverse[:])
 
-        probs_t = []
+        raised_t = []
         for h in range(HALVES):
-            flipped = psum.tile([P, M], BF16, name=f"probs_t_psum{h}")
-            nc.tensor.transpose(flipped[:], probs[:, h * P : (h + 1) * P], identity[:])
-            kept = held.tile([P, M], BF16, name=f"probs_t{h}")
+            flipped = psum.tile([P, M], BF16, name=f"raised_t_psum{h}")
+            nc.tensor.transpose(flipped[:], raised[:, h * P : (h + 1) * P], identity[:])
+            kept = held.tile([P, M], BF16, name=f"raised_t{h}")
             if h % 2 == 0:
                 nc.vector.tensor_copy(kept[:], flipped[:])
             else:
                 nc.scalar.copy(kept[:], flipped[:])
-            probs_t.append(kept)
+            raised_t.append(kept)
 
         result = psum.tile([M, D], F32, name="result")
         for h in range(HALVES):
             nc.tensor.matmul(
-                result[:], probs_t[h][:], values_t[:, h * D : (h + 1) * D], start=(h == 0), stop=(h == HALVES - 1)
+                result[:], raised_t[h][:], values_t[:, h * D : (h + 1) * D], start=(h == 0), stop=(h == HALVES - 1)
             )
 
         staged = held.tile([M, D], F32, name="staged")
-        nc.vector.tensor_copy(staged[:], result[:])
+        nc.vector.tensor_scalar_mul(staged[:], result[:], inverse[:])
         nc.sync.dma_start(out, staged[:])

@@ -34,14 +34,15 @@ def tile_nativesparseattentionlayer_kernel(tc, table, w, v, offs, out):
         scores = psum.tile([M, N], F32, name="scores")
         nc.tensor.matmul(scores[:], queries[:], keys[:].indirect(offsets[:]), start=True, stop=True)
 
-        top = held.tile([M, 1], F32, name="top")
-        nc.vector.reduce_max(top[:], scores[:], axis=mybir.AxisListType.X)
+        negated = held.tile([M, N], F32, name="negated")
         shift = held.tile([M, 1], F32, name="shift")
-        nc.vector.tensor_scalar_mul(shift[:], top[:], -SCALE)
+        nc.vector.tensor_scalar(
+            negated[:], scores[:], -SCALE, None, op0=mybir.AluOpType.mult, op1=mybir.AluOpType.min, accum_out=shift[:]
+        )
         raised = held.tile([M, N], BF16, name="raised")
         total = held.tile([M, 1], F32, name="total")
         nc.scalar.activation(
-            raised[:], scores[:], mybir.ActivationFunctionType.Exp, bias=shift[:], scale=SCALE, accum_out=total[:]
+            raised[:], negated[:], mybir.ActivationFunctionType.Exp, bias=shift[:], scale=-1.0, accum_out=total[:]
         )
 
         values_t_psum = psum.tile([P, HALVES * D], BF16, name="values_t_psum")

@@ -8,6 +8,8 @@ N = 256
 D = 128
 HALVES = N // P
 SCALE = 0.125
+PIECES = 4
+PIECE = S // PIECES
 
 FLOPS = 2 * P * M * N + 2 * N * M * D
 
@@ -19,12 +21,14 @@ U16 = mybir.dt.uint16
 def tile_nativesparseattentionlayer_kernel(tc, table, w, v, offs, out):
     nc = tc.nc
     with tc.tile_pool(name="held", bufs=1) as held, tc.psum_pool(name="psum", bufs=1) as psum:
-        keys = held.tile([P, S], BF16, name="keys")
-        nc.scalar.dma_start(keys[:], table)
         offsets = held.tile([P, N // 16], U16, name="offsets")
         nc.sync.dma_start(offsets[:], offs)
+        keys = held.tile([P, S], BF16, name="keys")
+        for i in range(PIECES):
+            queue = nc.scalar if i % 2 == 0 else nc.sync
+            queue.dma_start(keys[:, i * PIECE : (i + 1) * PIECE], table[:, i * PIECE : (i + 1) * PIECE])
         queries = held.tile([P, M], BF16, name="queries")
-        nc.sync.dma_start(queries[:], w)
+        nc.scalar.dma_start(queries[:], w)
         values = held.tile([P, N], BF16, name="values")
         nc.gpsimd.dma_start(values[:], v)
 

@@ -8,8 +8,6 @@ N = 256
 D = 128
 HALVES = N // P
 SCALE = 0.125
-PIECES = 4
-PIECE = S // PIECES
 
 FLOPS = 2 * P * M * N + 2 * N * M * D
 
@@ -21,14 +19,12 @@ U16 = mybir.dt.uint16
 def tile_nativesparseattentionlayer_kernel(tc, table, w, v, offs, out):
     nc = tc.nc
     with tc.tile_pool(name="held", bufs=1) as held, tc.psum_pool(name="psum", bufs=1) as psum:
+        keys = held.tile([P, S], BF16, name="keys")
+        nc.scalar.dma_start(keys[:], table)
         offsets = held.tile([P, N // 16], U16, name="offsets")
         nc.sync.dma_start(offsets[:], offs)
-        keys = held.tile([P, S], BF16, name="keys")
-        for i in range(PIECES):
-            queue = nc.scalar if i % 2 == 0 else nc.sync
-            queue.dma_start(keys[:, i * PIECE : (i + 1) * PIECE], table[:, i * PIECE : (i + 1) * PIECE])
         queries = held.tile([P, M], BF16, name="queries")
-        nc.scalar.dma_start(queries[:], w)
+        nc.sync.dma_start(queries[:], w)
         values = held.tile([P, N], BF16, name="values")
         nc.gpsimd.dma_start(values[:], v)
 
@@ -43,7 +39,7 @@ def tile_nativesparseattentionlayer_kernel(tc, table, w, v, offs, out):
         nc.vector.tensor_scalar(
             negated[:], scores[:], -SCALE, None, op0=mybir.AluOpType.mult, op1=mybir.AluOpType.min, accum_out=shift[:]
         )
-        raised = held.tile([M, N], BF16, name="raised")
+        raised = held.tile([M, N], F32, name="raised")
         total = held.tile([M, 1], F32, name="total")
         nc.scalar.activation(
             raised[:], negated[:], mybir.ActivationFunctionType.Exp, bias=shift[:], scale=-1.0, accum_out=total[:]
@@ -57,24 +53,26 @@ def tile_nativesparseattentionlayer_kernel(tc, table, w, v, offs, out):
 
         inverse = held.tile([M, 1], F32, name="inverse")
         nc.vector.reciprocal(inverse[:], total[:])
+        probs = held.tile([M, N], BF16, name="probs")
+        nc.vector.tensor_scalar_mul(probs[:], raised[:], inverse[:])
 
-        raised_t = []
+        probs_t = []
         for h in range(HALVES):
-            flipped = psum.tile([P, M], BF16, name=f"raised_t_psum{h}")
-            nc.tensor.transpose(flipped[:], raised[:, h * P : (h + 1) * P], identity[:])
-            kept = held.tile([P, M], BF16, name=f"raised_t{h}")
+            flipped = psum.tile([P, M], BF16, name=f"probs_t_psum{h}")
+            nc.tensor.transpose(flipped[:], probs[:, h * P : (h + 1) * P], identity[:])
+            kept = held.tile([P, M], BF16, name=f"probs_t{h}")
             if h % 2 == 0:
                 nc.vector.tensor_copy(kept[:], flipped[:])
             else:
                 nc.scalar.copy(kept[:], flipped[:])
-            raised_t.append(kept)
+            probs_t.append(kept)
 
         result = psum.tile([M, D], F32, name="result")
         for h in range(HALVES):
             nc.tensor.matmul(
-                result[:], raised_t[h][:], values_t[:, h * D : (h + 1) * D], start=(h == 0), stop=(h == HALVES - 1)
+                result[:], probs_t[h][:], values_t[:, h * D : (h + 1) * D], start=(h == 0), stop=(h == HALVES - 1)
             )
 
         staged = held.tile([M, D], F32, name="staged")
-        nc.vector.tensor_scalar_mul(staged[:], result[:], inverse[:])
+        nc.vector.tensor_copy(staged[:], result[:])
         nc.sync.dma_start(out, staged[:])

@@ -26,7 +26,7 @@ def tile_nativesparseattentionlayer_kernel(tc, table, w, v, offs, out):
         queries = held.tile([P, M], BF16, name="queries")
         nc.sync.dma_start(queries[:], w)
         values = held.tile([P, N], BF16, name="values")
-        nc.gpsimd.dma_start(values[:], v)
+        nc.scalar.dma_start(values[:], v)
 
         identity = held.tile([P, P], BF16, name="identity")
         make_identity(nc, identity[:])
@@ -39,7 +39,7 @@ def tile_nativesparseattentionlayer_kernel(tc, table, w, v, offs, out):
         nc.vector.tensor_scalar(
             negated[:], scores[:], -SCALE, None, op0=mybir.AluOpType.mult, op1=mybir.AluOpType.min, accum_out=shift[:]
         )
-        raised = held.tile([M, N], F32, name="raised")
+        raised = held.tile([M, N], BF16, name="raised")
         total = held.tile([M, 1], F32, name="total")
         nc.scalar.activation(
             raised[:], negated[:], mybir.ActivationFunctionType.Exp, bias=shift[:], scale=-1.0, accum_out=total[:]
@@ -53,26 +53,24 @@ def tile_nativesparseattentionlayer_kernel(tc, table, w, v, offs, out):
 
         inverse = held.tile([M, 1], F32, name="inverse")
         nc.vector.reciprocal(inverse[:], total[:])
-        probs = held.tile([M, N], BF16, name="probs")
-        nc.vector.tensor_scalar_mul(probs[:], raised[:], inverse[:])
 
-        probs_t = []
+        raised_t = []
         for h in range(HALVES):
-            flipped = psum.tile([P, M], BF16, name=f"probs_t_psum{h}")
-            nc.tensor.transpose(flipped[:], probs[:, h * P : (h + 1) * P], identity[:])
-            kept = held.tile([P, M], BF16, name=f"probs_t{h}")
+            flipped = psum.tile([P, M], BF16, name=f"raised_t_psum{h}")
+            nc.tensor.transpose(flipped[:], raised[:, h * P : (h + 1) * P], identity[:])
+            kept = held.tile([P, M], BF16, name=f"raised_t{h}")
             if h % 2 == 0:
                 nc.vector.tensor_copy(kept[:], flipped[:])
             else:
                 nc.scalar.copy(kept[:], flipped[:])
-            probs_t.append(kept)
+            raised_t.append(kept)
 
         result = psum.tile([M, D], F32, name="result")
         for h in range(HALVES):
             nc.tensor.matmul(
-                result[:], probs_t[h][:], values_t[:, h * D : (h + 1) * D], start=(h == 0), stop=(h == HALVES - 1)
+                result[:], raised_t[h][:], values_t[:, h * D : (h + 1) * D], start=(h == 0), stop=(h == HALVES - 1)
             )
 
         staged = held.tile([M, D], F32, name="staged")
-        nc.vector.tensor_copy(staged[:], result[:])
+        nc.vector.tensor_scalar_mul(staged[:], result[:], inverse[:])
         nc.sync.dma_start(out, staged[:])

@@ -59,10 +59,7 @@ def tile_nativesparseattentionlayer_kernel(tc, table, w, v, offs, out):
             flipped = psum.tile([P, M], BF16, name=f"raised_t_psum{h}")
             nc.tensor.transpose(flipped[:], raised[:, h * P : (h + 1) * P], identity[:])
             kept = held.tile([P, M], BF16, name=f"raised_t{h}")
-            if h % 2 == 0:
-                nc.vector.tensor_copy(kept[:], flipped[:])
-            else:
-                nc.scalar.copy(kept[:], flipped[:])
+            nc.vector.tensor_copy(kept[:], flipped[:])
             raised_t.append(kept)
 
         result = psum.tile([M, D], F32, name="result")

@@ -40,19 +40,22 @@ def tile_nativesparseattentionlayer_kernel(tc, table, w, v, offs, out):
             negated[:], scores[:], -SCALE, None, op0=mybir.AluOpType.mult, op1=mybir.AluOpType.min, accum_out=shift[:]
         )
         raised = held.tile([M, N], BF16, name="raised")
-        total = held.tile([M, 1], F32, name="total")
-        nc.scalar.activation(
-            raised[:], negated[:], mybir.ActivationFunctionType.Exp, bias=shift[:], scale=-1.0, accum_out=total[:]
-        )
+        half_totals = held.tile([M, HALVES], F32, name="half_totals")
+        for h in range(HALVES):
+            nc.scalar.activation(
+                raised[:, h * P : (h + 1) * P],
+                negated[:, h * P : (h + 1) * P],
+                mybir.ActivationFunctionType.Exp,
+                bias=shift[:],
+                scale=-1.0,
+                accum_out=half_totals[:, h : h + 1],
+            )
 
         values_t_psum = psum.tile([P, HALVES * D], BF16, name="values_t_psum")
         for h in range(HALVES):
             nc.tensor.transpose(values_t_psum[:, h * D : (h + 1) * D], values[:, h * P : (h + 1) * P], identity[:])
         values_t = held.tile([P, HALVES * D], BF16, name="values_t")
         nc.scalar.copy(values_t[:], values_t_psum[:])
-
-        inverse = held.tile([M, 1], F32, name="inverse")
-        nc.vector.reciprocal(inverse[:], total[:])
 
         raised_t = []
         for h in range(HALVES):
@@ -61,6 +64,11 @@ def tile_nativesparseattentionlayer_kernel(tc, table, w, v, offs, out):
             kept = held.tile([P, M], BF16, name=f"raised_t{h}")
             nc.vector.tensor_copy(kept[:], flipped[:])
             raised_t.append(kept)
+
+        total = held.tile([M, 1], F32, name="total")
+        nc.vector.tensor_reduce(total[:], half_totals[:], axis=mybir.AxisListType.X, op=mybir.AluOpType.add)
+        inverse = held.tile([M, 1], F32, name="inverse")
+        nc.vector.reciprocal(inverse[:], total[:])
 
         result = psum.tile([M, D], F32, name="result")
         for h in range(HALVES):

@@ -20,7 +20,7 @@ def tile_nativesparseattentionlayer_kernel(tc, table, w, v, offs, out):
     nc = tc.nc
     with tc.tile_pool(name="held", bufs=1) as held, tc.psum_pool(name="psum", bufs=1) as psum:
         keys = held.tile([P, S], BF16, name="keys")
-        nc.scalar.dma_start(keys[:], table)
+        nc.sync.dma_start(keys[:], table)
         offsets = held.tile([P, N // 16], U16, name="offsets")
         nc.sync.dma_start(offsets[:], offs)
         queries = held.tile([P, M], BF16, name="queries")

@@ -53,14 +53,16 @@ def tile_nativesparseattentionlayer_kernel(tc, table, w, v, offs, out):
 
         values_t_psum = psum.tile([P, HALVES * D], BF16, name="values_t_psum")
         for h in range(HALVES):
-            nc.tensor.transpose(values_t_psum[:, h * D : (h + 1) * D], values[:, h * P : (h + 1) * P], identity[:])
+            nc.tensor.matmul(
+                values_t_psum[:, h * D : (h + 1) * D], values[:, h * P : (h + 1) * P], identity[:], start=True, stop=True
+            )
         values_t = held.tile([P, HALVES * D], BF16, name="values_t")
         nc.scalar.copy(values_t[:], values_t_psum[:])
 
         raised_t = []
         for h in range(HALVES):
             flipped = psum.tile([P, M], BF16, name=f"raised_t_psum{h}")
-            nc.tensor.transpose(flipped[:], raised[:, h * P : (h + 1) * P], identity[:])
+            nc.tensor.matmul(flipped[:], raised[:, h * P : (h + 1) * P], identity[:], start=True, stop=True)
             kept = held.tile([P, M], BF16, name=f"raised_t{h}")
             nc.vector.tensor_copy(kept[:], flipped[:])
             raised_t.append(kept)

@@ -21,12 +21,12 @@ def tile_nativesparseattentionlayer_kernel(tc, table, w, v, offs, out):
     with tc.tile_pool(name="held", bufs=1) as held, tc.psum_pool(name="psum", bufs=1) as psum:
         keys = held.tile([P, S], BF16, name="keys")
         nc.sync.dma_start(keys[:], table)
+        queries = held.tile([P, M], BF16, name="queries")
+        nc.scalar.dma_start(queries[:], w)
         offsets = held.tile([P, N // 16], U16, name="offsets")
         nc.sync.dma_start(offsets[:], offs)
-        queries = held.tile([P, M], BF16, name="queries")
-        nc.sync.dma_start(queries[:], w)
         values = held.tile([P, N], BF16, name="values")
-        nc.scalar.dma_start(values[:], v)
+        nc.sync.dma_start(values[:], v)
 
         identity = held.tile([P, P], BF16, name="identity")
         make_identity(nc, identity[:])

import concourse.mybir as mybir
from concourse.masks import make_identity

P = 128
S = 1024
M = 128
N = 256
D = 128
HALVES = N // P
SCALE = 0.125

FLOPS = 2 * P * M * N + 2 * N * M * D

BF16 = mybir.dt.bfloat16
F32 = mybir.dt.float32
U16 = mybir.dt.uint16


def tile_nativesparseattentionlayer_kernel(tc, table, w, v, offs, out):
    nc = tc.nc
    with tc.tile_pool(name="held", bufs=1) as held, tc.psum_pool(name="psum", bufs=1) as psum:
        keys = held.tile([P, S], BF16, name="keys")
        nc.sync.dma_start(keys[:], table)
        queries = held.tile([P, M], BF16, name="queries")
        nc.scalar.dma_start(queries[:], w)
        offsets = held.tile([P, N // 16], U16, name="offsets")
        nc.sync.dma_start(offsets[:], offs)
        values = held.tile([P, N], BF16, name="values")
        nc.sync.dma_start(values[:], v)

        identity = held.tile([P, P], BF16, name="identity")
        make_identity(nc, identity[:])

        scores = psum.tile([M, N], F32, name="scores")
        nc.tensor.matmul(scores[:], queries[:], keys[:].indirect(offsets[:]), start=True, stop=True)

        negated = held.tile([M, N], F32, name="negated")
        shift = held.tile([M, 1], F32, name="shift")
        nc.vector.tensor_scalar(
            negated[:], scores[:], -SCALE, None, op0=mybir.AluOpType.mult, op1=mybir.AluOpType.min, accum_out=shift[:]
        )
        raised = held.tile([M, N], BF16, name="raised")
        half_totals = held.tile([M, HALVES], F32, name="half_totals")
        for h in range(HALVES):
            nc.scalar.activation(
                raised[:, h * P : (h + 1) * P],
                negated[:, h * P : (h + 1) * P],
                mybir.ActivationFunctionType.Exp,
                bias=shift[:],
                scale=-1.0,
                accum_out=half_totals[:, h : h + 1],
            )

        values_t_psum = psum.tile([P, HALVES * D], BF16, name="values_t_psum")
        for h in range(HALVES):
            nc.tensor.matmul(
                values_t_psum[:, h * D : (h + 1) * D], values[:, h * P : (h + 1) * P], identity[:], start=True, stop=True
            )
        values_t = held.tile([P, HALVES * D], BF16, name="values_t")
        nc.scalar.copy(values_t[:], values_t_psum[:])

        raised_t = []
        for h in range(HALVES):
            flipped = psum.tile([P, M], BF16, name=f"raised_t_psum{h}")
            nc.tensor.matmul(flipped[:], raised[:, h * P : (h + 1) * P], identity[:], start=True, stop=True)
            kept = held.tile([P, M], BF16, name=f"raised_t{h}")
            nc.vector.tensor_copy(kept[:], flipped[:])
            raised_t.append(kept)

        total = held.tile([M, 1], F32, name="total")
        nc.vector.tensor_reduce(total[:], half_totals[:], axis=mybir.AxisListType.X, op=mybir.AluOpType.add)
        inverse = held.tile([M, 1], F32, name="inverse")
        nc.vector.reciprocal(inverse[:], total[:])

        result = psum.tile([M, D], F32, name="result")
        for h in range(HALVES):
            nc.tensor.matmul(
                result[:], raised_t[h][:], values_t[:, h * D : (h + 1) * D], start=(h == 0), stop=(h == HALVES - 1)
            )

        staged = held.tile([M, D], F32, name="staged")
        nc.vector.tensor_scalar_mul(staged[:], result[:], inverse[:])
        nc.sync.dma_start(out, staged[:])
